import numpy as np
import ml_dtypes


def mxq(x, axis, fmt="e4m3"):
    dtype, down = {"e4m3": (ml_dtypes.float8_e4m3fn, 7), "e5m2": (ml_dtypes.float8_e5m2, 14)}[fmt]
    v = np.moveaxis(np.asarray(x, np.float32).astype(ml_dtypes.bfloat16).astype(np.float64), axis, -1)
    blocks = v.reshape(v.shape[:-1] + (-1, 32))
    amax = np.abs(blocks).max(-1, keepdims=True)
    byte = np.maximum(np.where(amax > 0, np.frexp(amax)[1] - 1 + 127, 0) - down, 1)
    scale = np.exp2(byte - 127.0)
    codes = (blocks / scale).astype(np.float32).astype(dtype).astype(np.float64)
    return np.moveaxis((codes * scale).reshape(v.shape), -1, axis)


WIDE = False


def mx_kscale(k):
    if not WIDE:
        return np.ones(k)
    levels = np.array([10, -10, 5, -5, 0])
    a = np.random.permutation(np.resize(levels, k // 512 * 4)).reshape(k // 512, 4)
    idx = np.arange(k)
    return np.exp2(a[idx // 512, idx % 128 // 32])


BF16 = ml_dtypes.bfloat16


def bf(x):
    return np.asarray(x, np.float32).astype(BF16)


def f64(x):
    return np.asarray(x).astype(np.float64)


NB, D1, KB, P, Q, LB, S = 4, 256, 8, 512, 512, 8, 512
D2 = KB * P
R = KB * Q // LB
DO = S * LB


def _blockdiag_butterfly_multiply(x, w1, w2):
    B, n = x.shape
    k, q, p = w1.shape
    l, s, r = w2.shape
    x_r = x.reshape(B, k, p).transpose(1, 0, 2)
    out1 = mxq(x_r, 2, "e4m3") @ mxq(w1, 2, "e4m3").transpose(0, 2, 1)
    out1 = out1.transpose(1, 0, 2).reshape(B, r, l).transpose(2, 0, 1)
    out2 = mxq(out1, 2, "e4m3") @ mxq(w2, 2, "e4m3").transpose(0, 2, 1)
    return out2.transpose(1, 2, 0).reshape(B, s * l)


def setup_inputs():
    s = mx_kscale(P)
    t = mx_kscale(R)
    tf = np.repeat(t, LB).reshape(KB, Q)
    return {"x": bf(np.random.standard_normal((NB, D1, D2)) * np.tile(s, KB)),
            "factorL": bf(np.random.standard_normal((KB, Q, P)) / np.sqrt(P) / s * tf[:, :, None]),
            "factorR": bf(np.random.standard_normal((LB, S, R)) / np.sqrt(R) / t),
            "bias": bf(np.random.standard_normal(DO) * 0.5)}


def reference(x, factorL, factorR, bias):
    b, d1, d2 = x.shape
    out = _blockdiag_butterfly_multiply(f64(x).reshape(-1, d2), f64(factorL), f64(factorR))
    out = out.reshape(b, d1, -1)
    return out + f64(bias)

@@ -1,0 +1,291 @@
+from contextlib import ExitStack
+
+import concourse.mybir as mybir
+from concourse.masks import make_identity
+
+F32 = mybir.dt.float32
+BF16 = mybir.dt.bfloat16
+U32 = mybir.dt.uint32
+I32 = mybir.dt.int32
+U8 = mybir.dt.uint8
+FP8X4 = mybir.dt.float8_e4m3fn_x4
+ADD = mybir.AluOpType.add
+MULT = mybir.AluOpType.mult
+
+P = 128
+TILES = 8
+FLOPS = 2 * 2 * 1024 * 8 * 512 * 512
+PIN = True
+W_BUFS = 8
+
+
+def tile_butterflyblocksparselinear_kernel(tc, x, factorL, factorR, bias, out):
+    nc = tc.nc
+    w_order = [("L", k) for k in range(8)] + [("R", l) for l in (4, 5, 6, 7, 0, 1, 2, 3)]
+    xf = x.flatten_outer_dims()
+    of = out.flatten_outer_dims()
+    with ExitStack() as ctx:
+        if PIN:
+            ctx.enter_context(tc.manual_schedule())
+        const = ctx.enter_context(tc.tile_pool(name="const", bufs=1))
+        xpool = ctx.enter_context(tc.tile_pool(name="xpool", bufs=3))
+        wpool = ctx.enter_context(tc.tile_pool(name="wpool", bufs=W_BUFS))
+        rpool = ctx.enter_context(tc.tile_pool(name="rpool", bufs=2))
+        gpool = ctx.enter_context(tc.tile_pool(name="gpool", bufs=3))
+        cpool = ctx.enter_context(tc.tile_pool(name="cpool", bufs=3))
+        opool = ctx.enter_context(tc.tile_pool(name="opool", bufs=8))
+        psum = ctx.enter_context(tc.psum_pool(name="psum", bufs=2))
+
+        ident_f = const.tile([P, P], F32, name="ident_f")
+        ident_b = const.tile([P, P], BF16, name="ident_b")
+        perm0 = const.tile([P, P], F32, name="perm0")
+        perm1 = const.tile([P, P], F32, name="perm1")
+        perms = [perm0, perm1]
+        bias_bc = const.tile([P, 4096], BF16, name="bias_bc")
+        l_codes = const.tile([P, 8, 512], U32, name="l_codes", align_bytes=64)
+        l_scales = const.tile([P, 8, 512], U8, name="l_scales", align_bytes=64)
+        r_codes = const.tile([P, 8, 512], U32, name="r_codes", align_bytes=64)
+        r_scales = const.tile([P, 8, 512], U8, name="r_scales", align_bytes=64)
+
+        g_tiles = [
+            const.tile([P, 2, 640], U32, name="g_codes0", align_bytes=64),
+            const.tile([P, 2, 640], U32, name="g_codes1", align_bytes=64),
+        ]
+        tmp = const.tile([P, 640], U32, name="tmp", align_bytes=64)
+        for g in g_tiles:
+            nc.vector.memset(g[:, :, 512:640].bitcast(I32), 0)
+
+        make_identity(nc, ident_f[:])
+        make_identity(nc, ident_b[:])
+        nc.vector.tensor_copy(
+            out=perm0[:].rearrange("p (h i) -> p h i", h=2), in_=ident_f[:].rearrange("p (i h) -> p h i", h=2)
+        )
+        nc.vector.tensor_copy(out=perm1[:, 0:64], in_=perm0[:, 64:128])
+        nc.vector.tensor_copy(out=perm1[:, 64:128], in_=perm0[:, 0:64])
+
+        xraw, xg, xc, xp, hg, gc, ob, wraw, live = {}, {}, {}, {}, {}, {}, {}, {}, {}
+        evac = {"S": nc.scalar.copy, "V": nc.vector.tensor_copy}
+
+        def load_x(t):
+            xraw[t] = xpool.tile([P, 4096], BF16, name="xraw")
+            nc.sync.dma_start(out=xraw[t][:], in_=xf[t * P : (t + 1) * P, :])
+
+        def load_w(i):
+            kind, j = w_order[i]
+            w = wpool.tile([P, 2048], BF16, name="wraw")
+            wraw[(kind, j)] = w
+            if kind == "L":
+                nc.sync.dma_start(out=w[:], in_=factorL[j].rearrange("(q a) p -> q (a p)", a=4))
+            else:
+                nc.sync.dma_start(
+                    out=w[:].rearrange("p (a r) -> p a r", a=4), in_=factorR[j].rearrange("(a s) r -> s a r", a=4)
+                )
+
+        def word_transposes(src_words, first_block, moving):
+            tp = psum.tile([P, 512], F32, name="tp", tag="tp")
+            for c in range(4):
+                b = first_block + c
+                nc.tensor.transpose(tp[:, c * P : (c + 1) * P], src_words[:, b * P : (b + 1) * P], moving[:])
+            return tp
+
+        def word_evac(eng, grouped, half, tp):
+            evac[eng](
+                out=grouped[:].bitcast(F32)[:, 512 * half : 512 * half + 512].rearrange("p (j c u) -> p j c u", j=2, u=2),
+                in_=tp[:].rearrange("p (j u c) -> p j c u", j=2, u=2),
+            )
+
+        def x_bank(t, bk, eng="S"):
+            if bk == 0:
+                xg[t] = gpool.tile([P, 4096], BF16, name="xg", bufs=2, align_bytes=64)
+            tp = word_transposes(xraw[t][:].bitcast(F32), 4 * bk, ident_f)
+            word_evac(eng, xg[t], bk, tp)
+
+        def quant_x(t, half):
+            if half == 0:
+                xc[t] = cpool.tile([P, 1024], U32, name="xc", align_bytes=64)
+                xp[t] = cpool.tile([P, 1024], U8, name="xp", align_bytes=64)
+            sl = slice(512 * half, 512 * half + 512)
+            nc.vector.quantize_mx(
+                out=xc[t][:, sl].bitcast(FP8X4), scales=xp[t][:, sl], in_=xg[t][:, 2048 * half : 2048 * half + 2048]
+            )
+
+        def l_block(k, engs):
+            wg = gpool.tile([P, 2048], BF16, name="wg", align_bytes=64)
+            live[("L", k)] = wg
+            for ah in range(2):
+                tp = word_transposes(wraw[("L", k)][:].bitcast(F32), 4 * ah, perms[k % 2])
+                word_evac(engs[ah], wg, ah, tp)
+
+        def quant_w(kind, j):
+            codes, scales = (l_codes, l_scales) if kind == "L" else (r_codes, r_scales)
+            nc.vector.quantize_mx(out=codes[:, j, :].bitcast(FP8X4), scales=scales[:, j, :], in_=live[(kind, j)][:])
+
+        def r_rotate(l):
+            ri = rpool.tile([P, 2048], BF16, name="ri")
+            live[("ri", l)] = ri
+            w = wraw[("R", l)]
+            for h in range(2):
+                nc.gpsimd.tensor_scalar(
+                    out=ri[:].rearrange("p (g c e) -> p g c e", g=8, e=2)[:, :, 64 * h : 64 * h + 64, :],
+                    in0=w[:].rearrange("p (g e c) -> p g c e", g=8, e=2)[:, :, 64 - 64 * h : 128 - 64 * h, :],
+                    scalar1=1.0,
+                    scalar2=0.0,
+                    op0=MULT,
+                    op1=ADD,
+                )
+
+        def r_block(l, engs):
+            wg = gpool.tile([P, 2048], BF16, name="wg", align_bytes=64)
+            live[("R", l)] = wg
+            for ah in range(2):
+                if l >= 4:
+                    tp = word_transposes(live[("ri", l)][:].bitcast(F32), 4 * ah, ident_f)
+                    word_evac(engs[ah], wg, ah, tp)
+                else:
+                    tp = psum.tile([P, 1024], BF16, name="tpb", tag="tp")
+                    for c in range(8):
+                        b = 8 * ah + c
+                        nc.tensor.transpose(tp[:, c * P : (c + 1) * P], wraw[("R", l)][:, b * P : (b + 1) * P], ident_b[:])
+                    evac[engs[ah]](
+                        out=wg[:, 1024 * ah : 1024 * ah + 1024].rearrange("p (a s t) -> p a s t", a=2, t=4),
+                        in_=tp[:].rearrange("p (a t s) -> p a s t", a=2, t=4),
+                    )
+
+        def h_bank(t, n, eng="S"):
+            rho, a = n // 4, n % 4
+            if a == 0:
+                hg[(t, rho)] = gpool.tile([P, 2048], BF16, name="hg", bufs=4, align_bytes=64)
+            hb = psum.tile([P, 512], F32, name="hb", tag="hb", bufs=3)
+            for tt in range(4):
+                k = 2 * tt + rho
+                nc.tensor.matmul_mx(
+                    out=hb[:, tt * P : (tt + 1) * P],
+                    lhsT=l_codes[:, k, a * P : (a + 1) * P].bitcast(FP8X4),
+                    lhsT_scale=l_scales[:, k, a * P : (a + 1) * P],
+                    rhs=xc[t][:, k * P : (k + 1) * P].bitcast(FP8X4),
+                    rhs_scale=xp[t][:, k * P : (k + 1) * P],
+                    start=True,
+                    stop=True,
+                )
+            evac[eng](
+                out=hg[(t, rho)][:, 512 * a : 512 * a + 512].rearrange("p (b t) -> p b t", t=4),
+                in_=hb[:].rearrange("p (t b) -> p b t", t=4),
+            )
+
+        def quant_g(t, rho):
+            gc[t] = g_tiles[t % 2]
+            nc.vector.quantize_mx(
+                out=gc[t][:, rho, 0:512].bitcast(FP8X4), scales=gc[t][:, rho, 512:640].bitcast(U8), in_=hg[(t, rho)][:]
+            )
+
+        def swap(t):
+            g = gc[t]
+            nc.vector.tensor_copy(out=tmp[64:128, :].bitcast(I32), in_=g[64:128, 0, :].bitcast(I32))
+            nc.vector.tensor_copy(out=g[64:128, 0, :].bitcast(I32), in_=g[64:128, 1, :].bitcast(I32))
+            nc.vector.tensor_copy(out=g[64:128, 1, :].bitcast(I32), in_=tmp[64:128, :].bitcast(I32))
+
+        def y_mm(t, n):
+            sg, lh = n // 2, n % 2
+            yb = psum.tile([P, 512], F32, name="yb", tag="yb", bufs=3)
+            live[("y", t, n)] = yb
+            for lam in range(4):
+                l = 4 * lh + lam
+                nc.tensor.matmul_mx(
+                    out=yb[:, lam * P : (lam + 1) * P],
+                    lhsT=gc[t][:, lh, lam * P : (lam + 1) * P].bitcast(FP8X4),
+                    lhsT_scale=gc[t][:, lh, 512 + 32 * lam : 544 + 32 * lam].bitcast(U8),
+                    rhs=r_codes[:, l, sg * P : (sg + 1) * P].bitcast(FP8X4),
+                    rhs_scale=r_scales[:, l, sg * P : (sg + 1) * P],
+                    start=True,
+                    stop=True,
+                )
+
+        def y_ev(t, n):
+            sg, lh = n // 2, n % 2
+            yb = live[("y", t, n)]
+            if lh == 0:
+                ob[(t, sg)] = opool.tile([P, 1024], F32, name="ob")
+            nc.vector.tensor_tensor(
+                out=ob[(t, sg)][:].rearrange("p (s l) -> p s l", l=8)[:, :, 4 * lh : 4 * lh + 4],
+                in0=yb[:].rearrange("p (l s) -> p s l", l=4),
+                in1=bias_bc[:, 1024 * sg : 1024 * sg + 1024].rearrange("p (s l) -> p s l", l=8)[:, :, 4 * lh : 4 * lh + 4],
+                op=ADD,
+            )
+            if lh == 1:
+                nc.sync.dma_start(out=of[t * P : (t + 1) * P, 1024 * sg : 1024 * sg + 1024], in_=ob[(t, sg)][:])
+
+        load_x(0)
+        for i in range(W_BUFS):
+            load_w(i)
+        for bk in range(4):
+            x_bank(0, bk)
+        quant_x(0, 0)
+        quant_x(0, 1)
+        for k in range(8):
+            l_block(k, ("S", "V") if k % 2 else ("S", "S"))
+            load_w(W_BUFS + k)
+            if k:
+                quant_w("L", k - 1)
+        quant_w("L", 7)
+        nc.sync.dma_start(out=bias_bc[:], in_=bias.partition_broadcast(P))
+        load_x(1)
+        load_x(2)
+        r_rotate(4)
+        r_rotate(5)
+        r_seq = (4, 0, 5, 1, 6, 2, 7, 3)
+        for n in range(8):
+            h_bank(0, n)
+            if n == 4:
+                quant_g(0, 0)
+            r_block(r_seq[n], ("S", "V"))
+            if n in (0, 2):
+                r_rotate(6 + n // 2)
+            if n:
+                quant_w("R", r_seq[n - 1])
+        quant_w("R", r_seq[7])
+        quant_g(0, 1)
+        for bk in range(4):
+            x_bank(1, bk)
+        load_x(3)
+        swap(0)
+        quant_x(1, 0)
+        quant_x(1, 1)
+        for bk in range(4):
+            x_bank(2, bk)
+        load_x(4)
+        for n in range(3):
+            y_mm(0, n)
+        for bk in range(4):
+            x_bank(3, bk)
+        quant_x(2, 0)
+        quant_x(2, 1)
+        for n in range(3):
+            y_ev(0, n)
+
+        for j in range(TILES):
+            if j + 5 < TILES:
+                load_x(j + 5)
+            nxt = j + 1 < TILES
+            if nxt:
+                for n in range(4):
+                    h_bank(j + 1, n)
+            for n in range(3, 8):
+                y_mm(j, n)
+                y_ev(j, n)
+                if nxt and n < 7:
+                    h_bank(j + 1, n + 1)
+            if j + 4 < TILES:
+                for bk in range(4):
+                    x_bank(j + 4, bk)
+            if nxt:
+                quant_g(j + 1, 0)
+                quant_g(j + 1, 1)
+                swap(j + 1)
+                for n in range(3):
+                    y_mm(j + 1, n)
+            if j + 3 < TILES:
+                quant_x(j + 3, 0)
+                quant_x(j + 3, 1)
+            if nxt:
+                for n in range(3):
+                    y_ev(j + 1, n)

@@ -17,6 +17,9 @@ TILES = 8
 FLOPS = 2 * 2 * 1024 * 8 * 512 * 512
 PIN = True
 W_BUFS = 8
+XWARM = 3
+WIN_DUMMIES = 3
+WARMUP = 8
 
 
 def tile_butterflyblocksparselinear_kernel(tc, x, factorL, factorR, bias, out):
@@ -30,11 +33,11 @@ def tile_butterflyblocksparselinear_kernel(tc, x, factorL, factorR, bias, out):
         const = ctx.enter_context(tc.tile_pool(name="const", bufs=1))
         xpool = ctx.enter_context(tc.tile_pool(name="xpool", bufs=3))
         wpool = ctx.enter_context(tc.tile_pool(name="wpool", bufs=W_BUFS))
-        rpool = ctx.enter_context(tc.tile_pool(name="rpool", bufs=2))
+        rpool = ctx.enter_context(tc.tile_pool(name="rpool", bufs=3))
         gpool = ctx.enter_context(tc.tile_pool(name="gpool", bufs=3))
         cpool = ctx.enter_context(tc.tile_pool(name="cpool", bufs=3))
         opool = ctx.enter_context(tc.tile_pool(name="opool", bufs=8))
-        psum = ctx.enter_context(tc.psum_pool(name="psum", bufs=2))
+        psum = ctx.enter_context(tc.psum_pool(name="psum", bufs=8))
 
         ident_f = const.tile([P, P], F32, name="ident_f")
         ident_b = const.tile([P, P], BF16, name="ident_b")
@@ -54,6 +57,13 @@ def tile_butterflyblocksparselinear_kernel(tc, x, factorL, factorR, bias, out):
         tmp = const.tile([P, 640], U32, name="tmp", align_bytes=64)
         for g in g_tiles:
             nc.vector.memset(g[:, :, 512:640].bitcast(I32), 0)
+
+        ones_b = const.tile([P, P], BF16, name="ones_b")
+        zeros_b = const.tile([P, 512], BF16, name="zeros_b")
+        nc.vector.memset(ones_b[:], 1.0)
+        nc.vector.memset(zeros_b[:], 0.0)
+        bias_row = xpool.tile([P, 4096], BF16, name="xraw")
+        nc.vector.memset(bias_row[:], 0.0)
 
         make_identity(nc, ident_f[:])
         make_identity(nc, ident_b[:])
@@ -81,8 +91,10 @@ def tile_butterflyblocksparselinear_kernel(tc, x, factorL, factorR, bias, out):
                     out=w[:].rearrange("p (a r) -> p a r", a=4), in_=factorR[j].rearrange("(a s) r -> s a r", a=4)
                 )
 
-        def word_transposes(src_words, first_block, moving):
-            tp = psum.tile([P, 512], F32, name="tp", tag="tp")
+        def word_transposes(src_words, first_block, moving, warm=False):
+            tp = psum.tile([P, 512], F32, name="tp", tag="ps")
+            if warm:
+                nc.tensor.matmul(out=tp[:], lhsT=ones_b[:], rhs=zeros_b[:], start=True, stop=True)
             for c in range(4):
                 b = first_block + c
                 nc.tensor.transpose(tp[:, c * P : (c + 1) * P], src_words[:, b * P : (b + 1) * P], moving[:])
@@ -97,7 +109,7 @@ def tile_butterflyblocksparselinear_kernel(tc, x, factorL, factorR, bias, out):
         def x_bank(t, bk, eng="S"):
             if bk == 0:
                 xg[t] = gpool.tile([P, 4096], BF16, name="xg", bufs=2, align_bytes=64)
-            tp = word_transposes(xraw[t][:].bitcast(F32), 4 * bk, ident_f)
+            tp = word_transposes(xraw[t][:].bitcast(F32), 4 * bk, ident_f, warm=(bk % 2 == 0) if t < XWARM else False)
             word_evac(eng, xg[t], bk, tp)
 
         def quant_x(t, half):
@@ -120,29 +132,28 @@ def tile_butterflyblocksparselinear_kernel(tc, x, factorL, factorR, bias, out):
             codes, scales = (l_codes, l_scales) if kind == "L" else (r_codes, r_scales)
             nc.vector.quantize_mx(out=codes[:, j, :].bitcast(FP8X4), scales=scales[:, j, :], in_=live[(kind, j)][:])
 
-        def r_rotate(l):
+        def r_rotate(l, eng="G"):
             ri = rpool.tile([P, 2048], BF16, name="ri")
             live[("ri", l)] = ri
             w = wraw[("R", l)]
             for h in range(2):
-                nc.gpsimd.tensor_scalar(
-                    out=ri[:].rearrange("p (g c e) -> p g c e", g=8, e=2)[:, :, 64 * h : 64 * h + 64, :],
-                    in0=w[:].rearrange("p (g e c) -> p g c e", g=8, e=2)[:, :, 64 - 64 * h : 128 - 64 * h, :],
-                    scalar1=1.0,
-                    scalar2=0.0,
-                    op0=MULT,
-                    op1=ADD,
-                )
+                dst = ri[:].rearrange("p (g c e) -> p g c e", g=8, e=2)[:, :, 64 * h : 64 * h + 64, :]
+                src = w[:].rearrange("p (g e c) -> p g c e", g=8, e=2)[:, :, 64 - 64 * h : 128 - 64 * h, :]
+                if eng == "G":
+                    nc.gpsimd.tensor_scalar(out=dst, in0=src, scalar1=1.0, scalar2=0.0, op0=MULT, op1=ADD)
+                else:
+                    nc.vector.tensor_copy(out=dst, in_=src)
 
         def r_block(l, engs):
             wg = gpool.tile([P, 2048], BF16, name="wg", align_bytes=64)
             live[("R", l)] = wg
             for ah in range(2):
                 if l >= 4:
-                    tp = word_transposes(live[("ri", l)][:].bitcast(F32), 4 * ah, ident_f)
+                    tp = word_transposes(live[("ri", l)][:].bitcast(F32), 4 * ah, ident_f, warm=ah == 0)
                     word_evac(engs[ah], wg, ah, tp)
                 else:
-                    tp = psum.tile([P, 1024], BF16, name="tpb", tag="tp")
+                    tp = psum.tile([P, 1024], BF16, name="tpb", tag="ps")
+                    nc.tensor.matmul(out=tp[:, 0:512], lhsT=ones_b[:], rhs=zeros_b[:], start=True, stop=True)
                     for c in range(8):
                         b = 8 * ah + c
                         nc.tensor.transpose(tp[:, c * P : (c + 1) * P], wraw[("R", l)][:, b * P : (b + 1) * P], ident_b[:])
@@ -155,7 +166,7 @@ def tile_butterflyblocksparselinear_kernel(tc, x, factorL, factorR, bias, out):
             rho, a = n // 4, n % 4
             if a == 0:
                 hg[(t, rho)] = gpool.tile([P, 2048], BF16, name="hg", bufs=4, align_bytes=64)
-            hb = psum.tile([P, 512], F32, name="hb", tag="hb", bufs=3)
+            hb = psum.tile([P, 512], F32, name="hb", tag="ps")
             for tt in range(4):
                 k = 2 * tt + rho
                 nc.tensor.matmul_mx(
@@ -186,8 +197,19 @@ def tile_butterflyblocksparselinear_kernel(tc, x, factorL, factorR, bias, out):
 
         def y_mm(t, n):
             sg, lh = n // 2, n % 2
-            yb = psum.tile([P, 512], F32, name="yb", tag="yb", bufs=3)
+            yb = psum.tile([P, 512], F32, name="yb", tag="ps")
             live[("y", t, n)] = yb
+            if n == 0:
+                for c in range(WIN_DUMMIES):
+                    nc.tensor.matmul_mx(
+                        out=yb[:],
+                        lhsT=l_codes[:, 0, 0:P].bitcast(FP8X4),
+                        lhsT_scale=l_scales[:, 0, 0:P],
+                        rhs=r_codes[:, 0, :].bitcast(FP8X4),
+                        rhs_scale=r_scales[:, 0, :],
+                        start=True,
+                        stop=True,
+                    )
             for lam in range(4):
                 l = 4 * lh + lam
                 nc.tensor.matmul_mx(
@@ -217,31 +239,49 @@ def tile_butterflyblocksparselinear_kernel(tc, x, factorL, factorR, bias, out):
         load_x(0)
         for i in range(W_BUFS):
             load_w(i)
+        nc.scalar.dma_start(out=bias_row[0:1, :], in_=bias.rearrange("(o n) -> o n", o=1))
+        warm_bank = psum.tile([P, 512], F32, name="warm_bank", tag="ps")
+        for c in range(WARMUP):
+            nc.tensor.matmul(out=warm_bank[:], lhsT=ones_b[:], rhs=zeros_b[:], start=True, stop=True)
+
+        def bias_chunk(c, eng):
+            if c % 2 == 0:
+                live["bias"] = psum.tile([P, 1024], BF16, name="tpb", tag="ps")
+            tp = live["bias"]
+            h = 512 * (c % 2)
+            nc.tensor.matmul(out=tp[:, h : h + 512], lhsT=ones_b[:], rhs=bias_row[:, 512 * c : 512 * c + 512], start=True, stop=True)
+            if c % 2:
+                evac[eng](out=bias_bc[:, 512 * (c - 1) : 512 * (c + 1)], in_=tp[:])
+
         for bk in range(4):
             x_bank(0, bk)
         quant_x(0, 0)
         quant_x(0, 1)
         for k in range(8):
-            l_block(k, ("S", "V") if k % 2 else ("S", "S"))
+            bias_chunk(k, "S")
+            l_block(k, ("S", "V"))
             load_w(W_BUFS + k)
             if k:
                 quant_w("L", k - 1)
         quant_w("L", 7)
-        nc.sync.dma_start(out=bias_bc[:], in_=bias.partition_broadcast(P))
         load_x(1)
-        load_x(2)
         r_rotate(4)
         r_rotate(5)
-        r_seq = (4, 0, 5, 1, 6, 2, 7, 3)
-        for n in range(8):
+        r_rotate(7, "V")
+        for n in range(4):
             h_bank(0, n)
+        r_seq = (4, 0, 1, 5, 2, 3, 7, 6)
+        for n in range(8):
             if n == 4:
-                quant_g(0, 0)
+                for m in range(4, 8):
+                    h_bank(0, m)
             r_block(r_seq[n], ("S", "V"))
-            if n in (0, 2):
-                r_rotate(6 + n // 2)
+            if n == 0:
+                r_rotate(6)
+                quant_g(0, 0)
             if n:
                 quant_w("R", r_seq[n - 1])
+        load_x(2)
         quant_w("R", r_seq[7])
         quant_g(0, 1)
         for bk in range(4):
@@ -249,22 +289,17 @@ def tile_butterflyblocksparselinear_kernel(tc, x, factorL, factorR, bias, out):
         load_x(3)
         swap(0)
         quant_x(1, 0)
-        quant_x(1, 1)
-        for bk in range(4):
-            x_bank(2, bk)
-        load_x(4)
         for n in range(3):
             y_mm(0, n)
         for bk in range(4):
-            x_bank(3, bk)
-        quant_x(2, 0)
-        quant_x(2, 1)
+            x_bank(2, bk)
+        quant_x(1, 1)
         for n in range(3):
             y_ev(0, n)
 
         for j in range(TILES):
-            if j + 5 < TILES:
-                load_x(j + 5)
+            if j + 4 < TILES:
+                load_x(j + 4)
             nxt = j + 1 < TILES
             if nxt:
                 for n in range(4):
@@ -272,20 +307,21 @@ def tile_butterflyblocksparselinear_kernel(tc, x, factorL, factorR, bias, out):
             for n in range(3, 8):
                 y_mm(j, n)
                 y_ev(j, n)
+                if n == 3 and j + 2 < TILES:
+                    quant_x(j + 2, 0)
                 if nxt and n < 7:
                     h_bank(j + 1, n + 1)
-            if j + 4 < TILES:
+            if j + 3 < TILES:
                 for bk in range(4):
-                    x_bank(j + 4, bk)
+                    x_bank(j + 3, bk)
             if nxt:
                 quant_g(j + 1, 0)
                 quant_g(j + 1, 1)
                 swap(j + 1)
                 for n in range(3):
                     y_mm(j + 1, n)
-            if j + 3 < TILES:
-                quant_x(j + 3, 0)
-                quant_x(j + 3, 1)
+            if j + 2 < TILES:
+                quant_x(j + 2, 1)
             if nxt:
                 for n in range(3):
                     y_ev(j + 1, n)

@@ -19,6 +19,7 @@ PIN = True
 W_BUFS = 8
 XWARM = 3
 WIN_DUMMIES = 3
+S_CHUNKS = (0,)
 WARMUP = 8
 
 
@@ -199,7 +200,7 @@ def tile_butterflyblocksparselinear_kernel(tc, x, factorL, factorR, bias, out):
             sg, lh = n // 2, n % 2
             yb = psum.tile([P, 512], F32, name="yb", tag="ps")
             live[("y", t, n)] = yb
-            if n == 0:
+            if n == 2:
                 for c in range(WIN_DUMMIES):
                     nc.tensor.matmul_mx(
                         out=yb[:],
@@ -227,14 +228,37 @@ def tile_butterflyblocksparselinear_kernel(tc, x, factorL, factorR, bias, out):
             yb = live[("y", t, n)]
             if lh == 0:
                 ob[(t, sg)] = opool.tile([P, 1024], F32, name="ob")
-            nc.vector.tensor_tensor(
-                out=ob[(t, sg)][:].rearrange("p (s l) -> p s l", l=8)[:, :, 4 * lh : 4 * lh + 4],
-                in0=yb[:].rearrange("p (l s) -> p s l", l=4),
-                in1=bias_bc[:, 1024 * sg : 1024 * sg + 1024].rearrange("p (s l) -> p s l", l=8)[:, :, 4 * lh : 4 * lh + 4],
-                op=ADD,
+            dst = ob[(t, sg)][:].rearrange("p (s l) -> p s l", l=8)[:, :, 4 * lh : 4 * lh + 4]
+            src = yb[:].rearrange("p (l s) -> p s l", l=4)
+            if sg in S_CHUNKS:
+                nc.scalar.copy(out=dst, in_=src)
+            else:
+                nc.vector.tensor_tensor(
+                    out=dst,
+                    in0=src,
+                    in1=bias_bc[:, 1024 * sg : 1024 * sg + 1024].rearrange("p (s l) -> p s l", l=8)[:, :, 4 * lh : 4 * lh + 4],
+                    op=ADD,
+                )
+
+        def g_bias(t, sg):
+            nc.gpsimd.tensor_tensor(
+                out=ob[(t, sg)][:], in0=ob[(t, sg)][:], in1=bias_bc[:, 1024 * sg : 1024 * sg + 1024], op=ADD
             )
-            if lh == 1:
-                nc.sync.dma_start(out=of[t * P : (t + 1) * P, 1024 * sg : 1024 * sg + 1024], in_=ob[(t, sg)][:])
+
+        def store(t, sg):
+            nc.sync.dma_start(out=of[t * P : (t + 1) * P, 1024 * sg : 1024 * sg + 1024], in_=ob[(t, sg)][:])
+
+        def y_head(t):
+            for n in (2, 3, 0, 1):
+                y_mm(t, n)
+
+        def y_head_out(t):
+            y_ev(t, 0)
+            y_ev(t, 1)
+            g_bias(t, 0)
+            y_ev(t, 2)
+            y_ev(t, 3)
+            store(t, 1)
 
         load_x(0)
         for i in range(W_BUFS):
@@ -259,12 +283,13 @@ def tile_butterflyblocksparselinear_kernel(tc, x, factorL, factorR, bias, out):
         quant_x(0, 1)
         for k in range(8):
             bias_chunk(k, "S")
-            l_block(k, ("S", "V"))
+            l_block(k, ("S", "V") if k > 1 else ("S", "S"))
             load_w(W_BUFS + k)
             if k:
                 quant_w("L", k - 1)
         quant_w("L", 7)
         load_x(1)
+        load_x(2)
         r_rotate(4)
         r_rotate(5)
         r_rotate(7, "V")
@@ -281,21 +306,18 @@ def tile_butterflyblocksparselinear_kernel(tc, x, factorL, factorR, bias, out):
                 quant_g(0, 0)
             if n:
                 quant_w("R", r_seq[n - 1])
-        load_x(2)
         quant_w("R", r_seq[7])
         quant_g(0, 1)
         for bk in range(4):
             x_bank(1, bk)
         load_x(3)
-        swap(0)
-        quant_x(1, 0)
-        for n in range(3):
-            y_mm(0, n)
         for bk in range(4):
             x_bank(2, bk)
+        swap(0)
+        quant_x(1, 0)
+        y_head(0)
         quant_x(1, 1)
-        for n in range(3):
-            y_ev(0, n)
+        y_head_out(0)
 
         for j in range(TILES):
             if j + 4 < TILES:
@@ -304,13 +326,17 @@ def tile_butterflyblocksparselinear_kernel(tc, x, factorL, factorR, bias, out):
             if nxt:
                 for n in range(4):
                     h_bank(j + 1, n)
-            for n in range(3, 8):
+            for n in range(4, 8):
                 y_mm(j, n)
                 y_ev(j, n)
-                if n == 3 and j + 2 < TILES:
+                if n == 6 and j + 2 < TILES:
                     quant_x(j + 2, 0)
-                if nxt and n < 7:
-                    h_bank(j + 1, n + 1)
+                if n == 5:
+                    store(j, 2)
+                    store(j, 0)
+                if nxt:
+                    h_bank(j + 1, n)
+            store(j, 3)
             if j + 3 < TILES:
                 for bk in range(4):
                     x_bank(j + 3, bk)
@@ -318,10 +344,8 @@ def tile_butterflyblocksparselinear_kernel(tc, x, factorL, factorR, bias, out):
                 quant_g(j + 1, 0)
                 quant_g(j + 1, 1)
                 swap(j + 1)
-                for n in range(3):
-                    y_mm(j + 1, n)
+                y_head(j + 1)
             if j + 2 < TILES:
                 quant_x(j + 2, 1)
             if nxt:
-                for n in range(3):
-                    y_ev(j + 1, n)
+                y_head_out(j + 1)

@@ -17,10 +17,13 @@ TILES = 8
 FLOPS = 2 * 2 * 1024 * 8 * 512 * 512
 PIN = True
 W_BUFS = 8
-XWARM = 3
+XWARM = 4
 WIN_DUMMIES = 3
 S_CHUNKS = (0,)
-WARMUP = 8
+WARMUP = 12
+X1E = "SSSS"
+X2E = "SSSS"
+H1E = "SVSVSVSV"
 
 
 def tile_butterflyblocksparselinear_kernel(tc, x, factorL, factorR, bias, out):
@@ -37,7 +40,7 @@ def tile_butterflyblocksparselinear_kernel(tc, x, factorL, factorR, bias, out):
         rpool = ctx.enter_context(tc.tile_pool(name="rpool", bufs=3))
         gpool = ctx.enter_context(tc.tile_pool(name="gpool", bufs=3))
         cpool = ctx.enter_context(tc.tile_pool(name="cpool", bufs=3))
-        opool = ctx.enter_context(tc.tile_pool(name="opool", bufs=8))
+        opool = ctx.enter_context(tc.tile_pool(name="opool", bufs=7))
         psum = ctx.enter_context(tc.psum_pool(name="psum", bufs=8))
 
         ident_f = const.tile([P, P], F32, name="ident_f")
@@ -56,15 +59,15 @@ def tile_butterflyblocksparselinear_kernel(tc, x, factorL, factorR, bias, out):
             const.tile([P, 2, 640], U32, name="g_codes1", align_bytes=64),
         ]
         tmp = const.tile([P, 640], U32, name="tmp", align_bytes=64)
-        for g in g_tiles:
-            nc.vector.memset(g[:, :, 512:640].bitcast(I32), 0)
-
         ones_b = const.tile([P, P], BF16, name="ones_b")
         zeros_b = const.tile([P, 512], BF16, name="zeros_b")
         nc.vector.memset(ones_b[:], 1.0)
         nc.vector.memset(zeros_b[:], 0.0)
-        bias_row = xpool.tile([P, 4096], BF16, name="xraw")
-        nc.vector.memset(bias_row[:], 0.0)
+        bias_row = const.tile([P, 4096], BF16, name="bias_row")
+        nc.vector.memset(bias_row[:].bitcast(I32), 0)
+        for g in g_tiles:
+            nc.vector.memset(g[:, :, 512:640].bitcast(I32), 0)
+
 
         make_identity(nc, ident_f[:])
         make_identity(nc, ident_b[:])
@@ -126,7 +129,7 @@ def tile_butterflyblocksparselinear_kernel(tc, x, factorL, factorR, bias, out):
             wg = gpool.tile([P, 2048], BF16, name="wg", align_bytes=64)
             live[("L", k)] = wg
             for ah in range(2):
-                tp = word_transposes(wraw[("L", k)][:].bitcast(F32), 4 * ah, perms[k % 2])
+                tp = word_transposes(wraw[("L", k)][:].bitcast(F32), 4 * ah, perms[k % 2], warm=ah == 0)
                 word_evac(engs[ah], wg, ah, tp)
 
         def quant_w(kind, j):
@@ -154,7 +157,8 @@ def tile_butterflyblocksparselinear_kernel(tc, x, factorL, factorR, bias, out):
                     word_evac(engs[ah], wg, ah, tp)
                 else:
                     tp = psum.tile([P, 1024], BF16, name="tpb", tag="ps")
-                    nc.tensor.matmul(out=tp[:, 0:512], lhsT=ones_b[:], rhs=zeros_b[:], start=True, stop=True)
+                    if ah == 0:
+                        nc.tensor.matmul(out=tp[:, 0:512], lhsT=ones_b[:], rhs=zeros_b[:], start=True, stop=True)
                     for c in range(8):
                         b = 8 * ah + c
                         nc.tensor.transpose(tp[:, c * P : (c + 1) * P], wraw[("R", l)][:, b * P : (b + 1) * P], ident_b[:])
@@ -249,16 +253,8 @@ def tile_butterflyblocksparselinear_kernel(tc, x, factorL, factorR, bias, out):
             nc.sync.dma_start(out=of[t * P : (t + 1) * P, 1024 * sg : 1024 * sg + 1024], in_=ob[(t, sg)][:])
 
         def y_head(t):
-            for n in (2, 3, 0, 1):
+            for n in (2, 0, 1):
                 y_mm(t, n)
-
-        def y_head_out(t):
-            y_ev(t, 0)
-            y_ev(t, 1)
-            g_bias(t, 0)
-            y_ev(t, 2)
-            y_ev(t, 3)
-            store(t, 1)
 
         load_x(0)
         for i in range(W_BUFS):
@@ -282,8 +278,7 @@ def tile_butterflyblocksparselinear_kernel(tc, x, factorL, factorR, bias, out):
         quant_x(0, 0)
         quant_x(0, 1)
         for k in range(8):
-            bias_chunk(k, "S")
-            l_block(k, ("S", "V") if k > 1 else ("S", "S"))
+            l_block(k, ("S", "V") if k % 2 else ("S", "S"))
             load_w(W_BUFS + k)
             if k:
                 quant_w("L", k - 1)
@@ -309,43 +304,52 @@ def tile_butterflyblocksparselinear_kernel(tc, x, factorL, factorR, bias, out):
         quant_w("R", r_seq[7])
         quant_g(0, 1)
         for bk in range(4):
-            x_bank(1, bk)
+            x_bank(1, bk, X1E[bk])
         load_x(3)
-        for bk in range(4):
-            x_bank(2, bk)
-        swap(0)
         quant_x(1, 0)
-        y_head(0)
         quant_x(1, 1)
-        y_head_out(0)
+        swap(0)
+        for bk in range(4):
+            x_bank(2, bk, X2E[bk])
+        load_x(4)
+        for c in range(8):
+            bias_chunk(c, "S")
+        for n in range(8):
+            h_bank(1, n, H1E[n])
+        quant_x(2, 0)
+        quant_x(2, 1)
+        for bk in range(4):
+            x_bank(3, bk)
+        load_x(5)
+        y_head(0)
 
         for j in range(TILES):
-            if j + 4 < TILES:
-                load_x(j + 4)
-            nxt = j + 1 < TILES
-            if nxt:
-                for n in range(4):
-                    h_bank(j + 1, n)
-            for n in range(4, 8):
+            if j + 6 < TILES:
+                load_x(j + 6)
+            y_ev(j, 0)
+            y_ev(j, 1)
+            g_bias(j, 0)
+            y_ev(j, 2)
+            for n in range(3, 8):
                 y_mm(j, n)
                 y_ev(j, n)
-                if n == 6 and j + 2 < TILES:
-                    quant_x(j + 2, 0)
+                if n % 2:
+                    store(j, n // 2)
                 if n == 5:
-                    store(j, 2)
                     store(j, 0)
-                if nxt:
-                    h_bank(j + 1, n)
-            store(j, 3)
-            if j + 3 < TILES:
+                if j + 2 < TILES:
+                    h_bank(j + 2, n - 3)
+            if j + 2 < TILES:
+                for n in range(5, 8):
+                    h_bank(j + 2, n)
+            if j + 4 < TILES:
                 for bk in range(4):
-                    x_bank(j + 3, bk)
-            if nxt:
+                    x_bank(j + 4, bk)
+            if j + 1 < TILES:
                 quant_g(j + 1, 0)
                 quant_g(j + 1, 1)
                 swap(j + 1)
                 y_head(j + 1)
-            if j + 2 < TILES:
-                quant_x(j + 2, 1)
-            if nxt:
-                y_head_out(j + 1)
+            if j + 3 < TILES:
+                quant_x(j + 3, 0)
+                quant_x(j + 3, 1)

@@ -15,12 +15,14 @@ MULT = mybir.AluOpType.mult
 P = 128
 TILES = 8
 FLOPS = 2 * 2 * 1024 * 8 * 512 * 512
-PIN = True
+PIN = False
 W_BUFS = 8
 XWARM = 4
-WIN_DUMMIES = 3
+WIN_DUMMIES = 0
 S_CHUNKS = (0,)
 WARMUP = 12
+R_SEQ = (4, 0, 1, 5, 2, 3, 7, 6)
+G_NEXT = (6,)
 X1E = "SSSS"
 X2E = "SSSS"
 H1E = "SVSVSVSV"
@@ -63,8 +65,6 @@ def tile_butterflyblocksparselinear_kernel(tc, x, factorL, factorR, bias, out):
         zeros_b = const.tile([P, 512], BF16, name="zeros_b")
         nc.vector.memset(ones_b[:], 1.0)
         nc.vector.memset(zeros_b[:], 0.0)
-        bias_row = const.tile([P, 4096], BF16, name="bias_row")
-        nc.vector.memset(bias_row[:].bitcast(I32), 0)
         for g in g_tiles:
             nc.vector.memset(g[:, :, 512:640].bitcast(I32), 0)
 
@@ -142,7 +142,8 @@ def tile_butterflyblocksparselinear_kernel(tc, x, factorL, factorR, bias, out):
             w = wraw[("R", l)]
             for h in range(2):
                 dst = ri[:].rearrange("p (g c e) -> p g c e", g=8, e=2)[:, :, 64 * h : 64 * h + 64, :]
-                src = w[:].rearrange("p (g e c) -> p g c e", g=8, e=2)[:, :, 64 - 64 * h : 128 - 64 * h, :]
+                o = 64 - 64 * h if l >= 4 else 64 * h
+                src = w[:].rearrange("p (g e c) -> p g c e", g=8, e=2)[:, :, o : o + 64, :]
                 if eng == "G":
                     nc.gpsimd.tensor_scalar(out=dst, in0=src, scalar1=1.0, scalar2=0.0, op0=MULT, op1=ADD)
                 else:
@@ -152,7 +153,7 @@ def tile_butterflyblocksparselinear_kernel(tc, x, factorL, factorR, bias, out):
             wg = gpool.tile([P, 2048], BF16, name="wg", align_bytes=64)
             live[("R", l)] = wg
             for ah in range(2):
-                if l >= 4:
+                if ("ri", l) in live:
                     tp = word_transposes(live[("ri", l)][:].bitcast(F32), 4 * ah, ident_f, warm=ah == 0)
                     word_evac(engs[ah], wg, ah, tp)
                 else:
@@ -259,46 +260,34 @@ def tile_butterflyblocksparselinear_kernel(tc, x, factorL, factorR, bias, out):
         load_x(0)
         for i in range(W_BUFS):
             load_w(i)
-        nc.scalar.dma_start(out=bias_row[0:1, :], in_=bias.rearrange("(o n) -> o n", o=1))
         warm_bank = psum.tile([P, 512], F32, name="warm_bank", tag="ps")
         for c in range(WARMUP):
             nc.tensor.matmul(out=warm_bank[:], lhsT=ones_b[:], rhs=zeros_b[:], start=True, stop=True)
-
-        def bias_chunk(c, eng):
-            if c % 2 == 0:
-                live["bias"] = psum.tile([P, 1024], BF16, name="tpb", tag="ps")
-            tp = live["bias"]
-            h = 512 * (c % 2)
-            nc.tensor.matmul(out=tp[:, h : h + 512], lhsT=ones_b[:], rhs=bias_row[:, 512 * c : 512 * c + 512], start=True, stop=True)
-            if c % 2:
-                evac[eng](out=bias_bc[:, 512 * (c - 1) : 512 * (c + 1)], in_=tp[:])
 
         for bk in range(4):
             x_bank(0, bk)
         quant_x(0, 0)
         quant_x(0, 1)
         for k in range(8):
-            l_block(k, ("S", "V") if k % 2 else ("S", "S"))
-            load_w(W_BUFS + k)
             if k:
                 quant_w("L", k - 1)
+            l_block(k, ("S", "V") if k % 2 else ("S", "S"))
+            load_w(W_BUFS + k)
         quant_w("L", 7)
         load_x(1)
         load_x(2)
         r_rotate(4)
         r_rotate(5)
         r_rotate(7, "V")
-        for n in range(4):
-            h_bank(0, n)
-        r_seq = (4, 0, 1, 5, 2, 3, 7, 6)
         for n in range(8):
-            if n == 4:
-                for m in range(4, 8):
-                    h_bank(0, m)
+            h_bank(0, n)
+        r_seq = R_SEQ
+        for n in range(8):
             r_block(r_seq[n], ("S", "V"))
             if n == 0:
-                r_rotate(6)
                 quant_g(0, 0)
+            if n < len(G_NEXT):
+                r_rotate(G_NEXT[n])
             if n:
                 quant_w("R", r_seq[n - 1])
         quant_w("R", r_seq[7])
@@ -306,14 +295,13 @@ def tile_butterflyblocksparselinear_kernel(tc, x, factorL, factorR, bias, out):
         for bk in range(4):
             x_bank(1, bk, X1E[bk])
         load_x(3)
+        nc.sync.dma_start(out=bias_bc[:], in_=bias.partition_broadcast(P))
         quant_x(1, 0)
         quant_x(1, 1)
         swap(0)
         for bk in range(4):
             x_bank(2, bk, X2E[bk])
         load_x(4)
-        for c in range(8):
-            bias_chunk(c, "S")
         for n in range(8):
             h_bank(1, n, H1E[n])
         quant_x(2, 0)

@@ -15,7 +15,7 @@ MULT = mybir.AluOpType.mult
 P = 128
 TILES = 8
 FLOPS = 2 * 2 * 1024 * 8 * 512 * 512
-PIN = False
+PIN = True
 W_BUFS = 8
 XWARM = 4
 WIN_DUMMIES = 0

@@ -21,6 +21,8 @@ XWARM = 4
 WIN_DUMMIES = 0
 S_CHUNKS = (0,)
 WARMUP = 12
+G_PIECES = 1
+ROT = "VVSV"
 R_SEQ = (4, 0, 1, 5, 2, 3, 7, 6)
 G_NEXT = (6,)
 X1E = "SSSS"
@@ -140,14 +142,16 @@ def tile_butterflyblocksparselinear_kernel(tc, x, factorL, factorR, bias, out):
             ri = rpool.tile([P, 2048], BF16, name="ri")
             live[("ri", l)] = ri
             w = wraw[("R", l)]
-            for h in range(2):
-                dst = ri[:].rearrange("p (g c e) -> p g c e", g=8, e=2)[:, :, 64 * h : 64 * h + 64, :]
-                o = 64 - 64 * h if l >= 4 else 64 * h
-                src = w[:].rearrange("p (g e c) -> p g c e", g=8, e=2)[:, :, o : o + 64, :]
-                if eng == "G":
-                    nc.gpsimd.tensor_scalar(out=dst, in0=src, scalar1=1.0, scalar2=0.0, op0=MULT, op1=ADD)
-                else:
-                    nc.vector.tensor_copy(out=dst, in_=src)
+            for gh in range(2 if eng == "G" else 1):
+                gs = slice(4 * gh, 4 * gh + 4) if eng == "G" else slice(0, 8)
+                for h in range(2):
+                    dst = ri[:].rearrange("p (g c e) -> p g c e", g=8, e=2)[:, gs, 64 * h : 64 * h + 64, :]
+                    o = 64 - 64 * h if l >= 4 else 64 * h
+                    src = w[:].rearrange("p (g e c) -> p g c e", g=8, e=2)[:, gs, o : o + 64, :]
+                    if eng == "G":
+                        nc.gpsimd.tensor_scalar(out=dst, in0=src, scalar1=1.0, scalar2=0.0, op0=MULT, op1=ADD)
+                    else:
+                        evac[eng](out=dst, in_=src)
 
         def r_block(l, engs):
             wg = gpool.tile([P, 2048], BF16, name="wg", align_bytes=64)
@@ -246,9 +250,14 @@ def tile_butterflyblocksparselinear_kernel(tc, x, factorL, factorR, bias, out):
                 )
 
         def g_bias(t, sg):
-            nc.gpsimd.tensor_tensor(
-                out=ob[(t, sg)][:], in0=ob[(t, sg)][:], in1=bias_bc[:, 1024 * sg : 1024 * sg + 1024], op=ADD
-            )
+            w = 1024 // G_PIECES
+            for c in range(G_PIECES):
+                nc.gpsimd.tensor_tensor(
+                    out=ob[(t, sg)][:, c * w : (c + 1) * w],
+                    in0=ob[(t, sg)][:, c * w : (c + 1) * w],
+                    in1=bias_bc[:, 1024 * sg + c * w : 1024 * sg + (c + 1) * w],
+                    op=ADD,
+                )
 
         def store(t, sg):
             nc.sync.dma_start(out=of[t * P : (t + 1) * P, 1024 * sg : 1024 * sg + 1024], in_=ob[(t, sg)][:])
@@ -276,9 +285,9 @@ def tile_butterflyblocksparselinear_kernel(tc, x, factorL, factorR, bias, out):
         quant_w("L", 7)
         load_x(1)
         load_x(2)
-        r_rotate(4)
-        r_rotate(5)
-        r_rotate(7, "V")
+        r_rotate(4, ROT[0])
+        r_rotate(5, ROT[1])
+        r_rotate(7, ROT[3])
         for n in range(8):
             h_bank(0, n)
         r_seq = R_SEQ
@@ -287,7 +296,7 @@ def tile_butterflyblocksparselinear_kernel(tc, x, factorL, factorR, bias, out):
             if n == 0:
                 quant_g(0, 0)
             if n < len(G_NEXT):
-                r_rotate(G_NEXT[n])
+                r_rotate(G_NEXT[n], ROT[2])
             if n:
                 quant_w("R", r_seq[n - 1])
         quant_w("R", r_seq[7])
@@ -316,14 +325,15 @@ def tile_butterflyblocksparselinear_kernel(tc, x, factorL, factorR, bias, out):
                 load_x(j + 6)
             y_ev(j, 0)
             y_ev(j, 1)
-            g_bias(j, 0)
+            if 0 in S_CHUNKS:
+                g_bias(j, 0)
             y_ev(j, 2)
             for n in range(3, 8):
                 y_mm(j, n)
                 y_ev(j, n)
                 if n % 2:
                     store(j, n // 2)
-                if n == 5:
+                if n == 7:
                     store(j, 0)
                 if j + 2 < TILES:
                     h_bank(j + 2, n - 3)

from contextlib import ExitStack

import concourse.mybir as mybir
from concourse.masks import make_identity

F32 = mybir.dt.float32
BF16 = mybir.dt.bfloat16
U32 = mybir.dt.uint32
I32 = mybir.dt.int32
U8 = mybir.dt.uint8
FP8X4 = mybir.dt.float8_e4m3fn_x4
ADD = mybir.AluOpType.add
MULT = mybir.AluOpType.mult

P = 128
TILES = 8
FLOPS = 2 * 2 * 1024 * 8 * 512 * 512
PIN = True
W_BUFS = 8
XWARM = 4
WIN_DUMMIES = 0
S_CHUNKS = (0,)
WARMUP = 12
G_PIECES = 1
ROT = "VVSV"
R_SEQ = (4, 0, 1, 5, 2, 3, 7, 6)
G_NEXT = (6,)
X1E = "SSSS"
X2E = "SSSS"
H1E = "SVSVSVSV"


def tile_butterflyblocksparselinear_kernel(tc, x, factorL, factorR, bias, out):
    nc = tc.nc
    w_order = [("L", k) for k in range(8)] + [("R", l) for l in (4, 5, 6, 7, 0, 1, 2, 3)]
    xf = x.flatten_outer_dims()
    of = out.flatten_outer_dims()
    with ExitStack() as ctx:
        if PIN:
            ctx.enter_context(tc.manual_schedule())
        const = ctx.enter_context(tc.tile_pool(name="const", bufs=1))
        xpool = ctx.enter_context(tc.tile_pool(name="xpool", bufs=3))
        wpool = ctx.enter_context(tc.tile_pool(name="wpool", bufs=W_BUFS))
        rpool = ctx.enter_context(tc.tile_pool(name="rpool", bufs=3))
        gpool = ctx.enter_context(tc.tile_pool(name="gpool", bufs=3))
        cpool = ctx.enter_context(tc.tile_pool(name="cpool", bufs=3))
        opool = ctx.enter_context(tc.tile_pool(name="opool", bufs=7))
        psum = ctx.enter_context(tc.psum_pool(name="psum", bufs=8))

        ident_f = const.tile([P, P], F32, name="ident_f")
        ident_b = const.tile([P, P], BF16, name="ident_b")
        perm0 = const.tile([P, P], F32, name="perm0")
        perm1 = const.tile([P, P], F32, name="perm1")
        perms = [perm0, perm1]
        bias_bc = const.tile([P, 4096], BF16, name="bias_bc")
        l_codes = const.tile([P, 8, 512], U32, name="l_codes", align_bytes=64)
        l_scales = const.tile([P, 8, 512], U8, name="l_scales", align_bytes=64)
        r_codes = const.tile([P, 8, 512], U32, name="r_codes", align_bytes=64)
        r_scales = const.tile([P, 8, 512], U8, name="r_scales", align_bytes=64)

        g_tiles = [
            const.tile([P, 2, 640], U32, name="g_codes0", align_bytes=64),
            const.tile([P, 2, 640], U32, name="g_codes1", align_bytes=64),
        ]
        tmp = const.tile([P, 640], U32, name="tmp", align_bytes=64)
        ones_b = const.tile([P, P], BF16, name="ones_b")
        zeros_b = const.tile([P, 512], BF16, name="zeros_b")
        nc.vector.memset(ones_b[:], 1.0)
        nc.vector.memset(zeros_b[:], 0.0)
        for g in g_tiles:
            nc.vector.memset(g[:, :, 512:640].bitcast(I32), 0)


        make_identity(nc, ident_f[:])
        make_identity(nc, ident_b[:])
        nc.vector.tensor_copy(
            out=perm0[:].rearrange("p (h i) -> p h i", h=2), in_=ident_f[:].rearrange("p (i h) -> p h i", h=2)
        )
        nc.vector.tensor_copy(out=perm1[:, 0:64], in_=perm0[:, 64:128])
        nc.vector.tensor_copy(out=perm1[:, 64:128], in_=perm0[:, 0:64])

        xraw, xg, xc, xp, hg, gc, ob, wraw, live = {}, {}, {}, {}, {}, {}, {}, {}, {}
        evac = {"S": nc.scalar.copy, "V": nc.vector.tensor_copy}

        def load_x(t):
            xraw[t] = xpool.tile([P, 4096], BF16, name="xraw")
            nc.sync.dma_start(out=xraw[t][:], in_=xf[t * P : (t + 1) * P, :])

        def load_w(i):
            kind, j = w_order[i]
            w = wpool.tile([P, 2048], BF16, name="wraw")
            wraw[(kind, j)] = w
            if kind == "L":
                nc.sync.dma_start(out=w[:], in_=factorL[j].rearrange("(q a) p -> q (a p)", a=4))
            else:
                nc.sync.dma_start(
                    out=w[:].rearrange("p (a r) -> p a r", a=4), in_=factorR[j].rearrange("(a s) r -> s a r", a=4)
                )

        def word_transposes(src_words, first_block, moving, warm=False):
            tp = psum.tile([P, 512], F32, name="tp", tag="ps")
            if warm:
                nc.tensor.matmul(out=tp[:], lhsT=ones_b[:], rhs=zeros_b[:], start=True, stop=True)
            for c in range(4):
                b = first_block + c
                nc.tensor.transpose(tp[:, c * P : (c + 1) * P], src_words[:, b * P : (b + 1) * P], moving[:])
            return tp

        def word_evac(eng, grouped, half, tp):
            evac[eng](
                out=grouped[:].bitcast(F32)[:, 512 * half : 512 * half + 512].rearrange("p (j c u) -> p j c u", j=2, u=2),
                in_=tp[:].rearrange("p (j u c) -> p j c u", j=2, u=2),
            )

        def x_bank(t, bk, eng="S"):
            if bk == 0:
                xg[t] = gpool.tile([P, 4096], BF16, name="xg", bufs=2, align_bytes=64)
            tp = word_transposes(xraw[t][:].bitcast(F32), 4 * bk, ident_f, warm=(bk % 2 == 0) if t < XWARM else False)
            word_evac(eng, xg[t], bk, tp)

        def quant_x(t, half):
            if half == 0:
                xc[t] = cpool.tile([P, 1024], U32, name="xc", align_bytes=64)
                xp[t] = cpool.tile([P, 1024], U8, name="xp", align_bytes=64)
            sl = slice(512 * half, 512 * half + 512)
            nc.vector.quantize_mx(
                out=xc[t][:, sl].bitcast(FP8X4), scales=xp[t][:, sl], in_=xg[t][:, 2048 * half : 2048 * half + 2048]
            )

        def l_block(k, engs):
            wg = gpool.tile([P, 2048], BF16, name="wg", align_bytes=64)
            live[("L", k)] = wg
            for ah in range(2):
                tp = word_transposes(wraw[("L", k)][:].bitcast(F32), 4 * ah, perms[k % 2], warm=ah == 0)
                word_evac(engs[ah], wg, ah, tp)

        def quant_w(kind, j):
            codes, scales = (l_codes, l_scales) if kind == "L" else (r_codes, r_scales)
            nc.vector.quantize_mx(out=codes[:, j, :].bitcast(FP8X4), scales=scales[:, j, :], in_=live[(kind, j)][:])

        def r_rotate(l, eng="G"):
            ri = rpool.tile([P, 2048], BF16, name="ri")
            live[("ri", l)] = ri
            w = wraw[("R", l)]
            for gh in range(2 if eng == "G" else 1):
                gs = slice(4 * gh, 4 * gh + 4) if eng == "G" else slice(0, 8)
                for h in range(2):
                    dst = ri[:].rearrange("p (g c e) -> p g c e", g=8, e=2)[:, gs, 64 * h : 64 * h + 64, :]
                    o = 64 - 64 * h if l >= 4 else 64 * h
                    src = w[:].rearrange("p (g e c) -> p g c e", g=8, e=2)[:, gs, o : o + 64, :]
                    if eng == "G":
                        nc.gpsimd.tensor_scalar(out=dst, in0=src, scalar1=1.0, scalar2=0.0, op0=MULT, op1=ADD)
                    else:
                        evac[eng](out=dst, in_=src)

        def r_block(l, engs):
            wg = gpool.tile([P, 2048], BF16, name="wg", align_bytes=64)
            live[("R", l)] = wg
            for ah in range(2):
                if ("ri", l) in live:
                    tp = word_transposes(live[("ri", l)][:].bitcast(F32), 4 * ah, ident_f, warm=ah == 0)
                    word_evac(engs[ah], wg, ah, tp)
                else:
                    tp = psum.tile([P, 1024], BF16, name="tpb", tag="ps")
                    if ah == 0:
                        nc.tensor.matmul(out=tp[:, 0:512], lhsT=ones_b[:], rhs=zeros_b[:], start=True, stop=True)
                    for c in range(8):
                        b = 8 * ah + c
                        nc.tensor.transpose(tp[:, c * P : (c + 1) * P], wraw[("R", l)][:, b * P : (b + 1) * P], ident_b[:])
                    evac[engs[ah]](
                        out=wg[:, 1024 * ah : 1024 * ah + 1024].rearrange("p (a s t) -> p a s t", a=2, t=4),
                        in_=tp[:].rearrange("p (a t s) -> p a s t", a=2, t=4),
                    )

        def h_bank(t, n, eng="S"):
            rho, a = n // 4, n % 4
            if a == 0:
                hg[(t, rho)] = gpool.tile([P, 2048], BF16, name="hg", bufs=4, align_bytes=64)
            hb = psum.tile([P, 512], F32, name="hb", tag="ps")
            for tt in range(4):
                k = 2 * tt + rho
                nc.tensor.matmul_mx(
                    out=hb[:, tt * P : (tt + 1) * P],
                    lhsT=l_codes[:, k, a * P : (a + 1) * P].bitcast(FP8X4),
                    lhsT_scale=l_scales[:, k, a * P : (a + 1) * P],
                    rhs=xc[t][:, k * P : (k + 1) * P].bitcast(FP8X4),
                    rhs_scale=xp[t][:, k * P : (k + 1) * P],
                    start=True,
                    stop=True,
                )
            evac[eng](
                out=hg[(t, rho)][:, 512 * a : 512 * a + 512].rearrange("p (b t) -> p b t", t=4),
                in_=hb[:].rearrange("p (t b) -> p b t", t=4),
            )

        def quant_g(t, rho):
            gc[t] = g_tiles[t % 2]
            nc.vector.quantize_mx(
                out=gc[t][:, rho, 0:512].bitcast(FP8X4), scales=gc[t][:, rho, 512:640].bitcast(U8), in_=hg[(t, rho)][:]
            )

        def swap(t):
            g = gc[t]
            nc.vector.tensor_copy(out=tmp[64:128, :].bitcast(I32), in_=g[64:128, 0, :].bitcast(I32))
            nc.vector.tensor_copy(out=g[64:128, 0, :].bitcast(I32), in_=g[64:128, 1, :].bitcast(I32))
            nc.vector.tensor_copy(out=g[64:128, 1, :].bitcast(I32), in_=tmp[64:128, :].bitcast(I32))

        def y_mm(t, n):
            sg, lh = n // 2, n % 2
            yb = psum.tile([P, 512], F32, name="yb", tag="ps")
            live[("y", t, n)] = yb
            if n == 2:
                for c in range(WIN_DUMMIES):
                    nc.tensor.matmul_mx(
                        out=yb[:],
                        lhsT=l_codes[:, 0, 0:P].bitcast(FP8X4),
                        lhsT_scale=l_scales[:, 0, 0:P],
                        rhs=r_codes[:, 0, :].bitcast(FP8X4),
                        rhs_scale=r_scales[:, 0, :],
                        start=True,
                        stop=True,
                    )
            for lam in range(4):
                l = 4 * lh + lam
                nc.tensor.matmul_mx(
                    out=yb[:, lam * P : (lam + 1) * P],
                    lhsT=gc[t][:, lh, lam * P : (lam + 1) * P].bitcast(FP8X4),
                    lhsT_scale=gc[t][:, lh, 512 + 32 * lam : 544 + 32 * lam].bitcast(U8),
                    rhs=r_codes[:, l, sg * P : (sg + 1) * P].bitcast(FP8X4),
                    rhs_scale=r_scales[:, l, sg * P : (sg + 1) * P],
                    start=True,
                    stop=True,
                )

        def y_ev(t, n):
            sg, lh = n // 2, n % 2
            yb = live[("y", t, n)]
            if lh == 0:
                ob[(t, sg)] = opool.tile([P, 1024], F32, name="ob")
            dst = ob[(t, sg)][:].rearrange("p (s l) -> p s l", l=8)[:, :, 4 * lh : 4 * lh + 4]
            src = yb[:].rearrange("p (l s) -> p s l", l=4)
            if sg in S_CHUNKS:
                nc.scalar.copy(out=dst, in_=src)
            else:
                nc.vector.tensor_tensor(
                    out=dst,
                    in0=src,
                    in1=bias_bc[:, 1024 * sg : 1024 * sg + 1024].rearrange("p (s l) -> p s l", l=8)[:, :, 4 * lh : 4 * lh + 4],
                    op=ADD,
                )

        def g_bias(t, sg):
            w = 1024 // G_PIECES
            for c in range(G_PIECES):
                nc.gpsimd.tensor_tensor(
                    out=ob[(t, sg)][:, c * w : (c + 1) * w],
                    in0=ob[(t, sg)][:, c * w : (c + 1) * w],
                    in1=bias_bc[:, 1024 * sg + c * w : 1024 * sg + (c + 1) * w],
                    op=ADD,
                )

        def store(t, sg):
            nc.sync.dma_start(out=of[t * P : (t + 1) * P, 1024 * sg : 1024 * sg + 1024], in_=ob[(t, sg)][:])

        def y_head(t):
            for n in (2, 0, 1):
                y_mm(t, n)

        load_x(0)
        for i in range(W_BUFS):
            load_w(i)
        warm_bank = psum.tile([P, 512], F32, name="warm_bank", tag="ps")
        for c in range(WARMUP):
            nc.tensor.matmul(out=warm_bank[:], lhsT=ones_b[:], rhs=zeros_b[:], start=True, stop=True)

        for bk in range(4):
            x_bank(0, bk)
        quant_x(0, 0)
        quant_x(0, 1)
        for k in range(8):
            if k:
                quant_w("L", k - 1)
            l_block(k, ("S", "V") if k % 2 else ("S", "S"))
            load_w(W_BUFS + k)
        quant_w("L", 7)
        load_x(1)
        load_x(2)
        r_rotate(4, ROT[0])
        r_rotate(5, ROT[1])
        r_rotate(7, ROT[3])
        for n in range(8):
            h_bank(0, n)
        r_seq = R_SEQ
        for n in range(8):
            r_block(r_seq[n], ("S", "V"))
            if n == 0:
                quant_g(0, 0)
            if n < len(G_NEXT):
                r_rotate(G_NEXT[n], ROT[2])
            if n:
                quant_w("R", r_seq[n - 1])
        quant_w("R", r_seq[7])
        quant_g(0, 1)
        for bk in range(4):
            x_bank(1, bk, X1E[bk])
        load_x(3)
        nc.sync.dma_start(out=bias_bc[:], in_=bias.partition_broadcast(P))
        quant_x(1, 0)
        quant_x(1, 1)
        swap(0)
        for bk in range(4):
            x_bank(2, bk, X2E[bk])
        load_x(4)
        for n in range(8):
            h_bank(1, n, H1E[n])
        quant_x(2, 0)
        quant_x(2, 1)
        for bk in range(4):
            x_bank(3, bk)
        load_x(5)
        y_head(0)

        for j in range(TILES):
            if j + 6 < TILES:
                load_x(j + 6)
            y_ev(j, 0)
            y_ev(j, 1)
            if 0 in S_CHUNKS:
                g_bias(j, 0)
            y_ev(j, 2)
            for n in range(3, 8):
                y_mm(j, n)
                y_ev(j, n)
                if n % 2:
                    store(j, n // 2)
                if n == 7:
                    store(j, 0)
                if j + 2 < TILES:
                    h_bank(j + 2, n - 3)
            if j + 2 < TILES:
                for n in range(5, 8):
                    h_bank(j + 2, n)
            if j + 4 < TILES:
                for bk in range(4):
                    x_bank(j + 4, bk)
            if j + 1 < TILES:
                quant_g(j + 1, 0)
                quant_g(j + 1, 1)
                swap(j + 1)
                y_head(j + 1)
            if j + 3 < TILES:
                quant_x(j + 3, 0)
                quant_x(j + 3, 1)
